import numpy as np
import ml_dtypes


def mxq(x, axis, fmt="e4m3"):
    dtype, down = {"e4m3": (ml_dtypes.float8_e4m3fn, 7), "e5m2": (ml_dtypes.float8_e5m2, 14)}[fmt]
    v = np.moveaxis(np.asarray(x, np.float32).astype(ml_dtypes.bfloat16).astype(np.float64), axis, -1)
    blocks = v.reshape(v.shape[:-1] + (-1, 32))
    amax = np.abs(blocks).max(-1, keepdims=True)
    byte = np.maximum(np.where(amax > 0, np.frexp(amax)[1] - 1 + 127, 0) - down, 1)
    scale = np.exp2(byte - 127.0)
    codes = (blocks / scale).astype(np.float32).astype(dtype).astype(np.float64)
    return np.moveaxis((codes * scale).reshape(v.shape), -1, axis)


WIDE = False


def mx_kscale(k):
    if not WIDE:
        return np.ones(k)
    levels = np.array([10, -10, 5, -5, 0])
    if k % 512:
        return np.exp2(np.random.permutation(np.resize(levels, k // 32))).repeat(32)
    a = np.empty((k // 512, 16))
    for p in range(k // 512):
        a[p, :8] = np.random.permutation(np.resize(levels, 8))
        for g in range(8):
            far = levels[np.abs(levels - a[p, g]) >= 10]
            a[p, g + 8] = far[np.random.randint(len(far))]
    return np.exp2(a.ravel()).repeat(32)


BF16 = ml_dtypes.bfloat16


def bf(x):
    return np.asarray(x, np.float32).astype(BF16)


def f64(x):
    return np.asarray(x).astype(np.float64)


B, L, D, H, DH = 4, 256, 1024, 16, 64
THETA = 100000.0
E = H * DH


def rope(t):
    pos = np.arange(L, dtype=np.float64)
    inv_freq = 1.0 / THETA ** (np.arange(0, DH, 2, dtype=np.float64) / DH)
    ang = pos[:, None] * inv_freq[None, :]
    cos = np.cos(ang)[:, :, None]
    sin = np.sin(ang)[:, :, None]
    tp = t.reshape(*t.shape[:-1], DH // 2, 2)
    x1, x2 = tp[..., 0], tp[..., 1]
    rot = np.stack([-x2, x1], axis=-1)
    out = tp * cos + rot * sin
    return out.reshape(*t.shape)


def draw0():
    s = mx_kscale(D)
    return {"x": bf(np.random.standard_normal((B, L, D)) * s),
            "W": bf(np.random.standard_normal((3 * E, D)) / np.sqrt(D) / s)}


def core(x, W):
    qkv = mxq(f64(x), 2, "e4m3") @ mxq(f64(W), 1, "e4m3").T
    qkv = qkv.reshape(B, L, 3, H, DH)
    qkv = np.transpose(qkv, (0, 3, 1, 2, 4))
    q, k, v = qkv[..., 0, :], qkv[..., 1, :], qkv[..., 2, :]
    return rope(q), rope(k), np.ascontiguousarray(v)


def e4m3fn_bytes(y):
    return np.clip(np.asarray(y, np.float64), -448.0, 448.0).astype(np.float32).astype(ml_dtypes.float8_e4m3fn).view(np.uint8)


def e4m3fn_values(b):
    return np.asarray(b, np.uint8).view(ml_dtypes.float8_e4m3fn).astype(np.float64)


def setup_inputs():
    d = draw0()
    x0 = np.asarray(d['W']).astype(np.float64)
    s = (np.max(np.abs(x0), axis=(0,), keepdims=True) / 448.0).astype(np.float32)
    out = {}
    for k, v in d.items():
        if k == 'W':
            out['W_bytes'] = e4m3fn_bytes(x0 / s.astype(np.float64))
            out['W_scale'] = s
        else:
            out[k] = v
    return out


def reference(x, W_bytes, W_scale):
    return core(x, e4m3fn_values(W_bytes) * W_scale.astype(np.float64))

@@ -1,0 +1,372 @@
+import math
+from contextlib import ExitStack
+
+import concourse.masks as masks
+import concourse.mybir as mybir
+
+F32 = mybir.dt.float32
+BF16 = mybir.dt.bfloat16
+I32 = mybir.dt.int32
+U32 = mybir.dt.uint32
+U8 = mybir.dt.uint8
+FP8 = mybir.dt.float8_e4m3fn
+FP8X4 = mybir.dt.float8_e4m3fn_x4
+ALU = mybir.AluOpType
+ACTF = mybir.ActivationFunctionType
+
+B, L, D, H, DH = 4, 256, 1024, 16, 64
+THETA = 100000.0
+FLOPS = 2 * B * L * D * 3 * H * DH
+
+P = 128
+NG = 12
+SEQ = (0, 4, 1, 5, 8, 2, 6, 3, 9, 10, 7, 11)
+UNITS = ((0,), (1,), (2,), (3, 4), (5,), (6, 7), (8, 9), (10,), (11,))
+MANUAL = True
+SCALE_ON_ACT = ()
+KIND = (0, 1, 0, 0, 1, 0, 1, 0)
+KIND_END = (0, 0, 2, 2)
+LEAD_MM = 2
+SPLIT_CASTS = 2
+LEAD_T = 2
+LEAD_C = 3
+LEAD_P = 4
+TP_BUFS = 4
+ACC_BUFS = 4
+
+TWO_PI = 2.0 * math.pi
+C1 = 6.28125
+C2 = 0.0019352436065673828
+C3 = TWO_PI - C1 - C2
+
+
+def tile_multiheadselfattention_pa_kernel(tc, x, W_bytes, W_scale, out_0, out_1, out_2):
+    nc = tc.nc
+    outs = (out_0, out_1, out_2)
+
+    with ExitStack() as ctx:
+        const = ctx.enter_context(tc.tile_pool(name="const", bufs=1))
+        wbfp = ctx.enter_context(tc.tile_pool(name="wbfp", bufs=4))
+        wgp = ctx.enter_context(tc.tile_pool(name="wgp", bufs=2))
+        wcp = ctx.enter_context(tc.tile_pool(name="wcp", bufs=3))
+        stp = ctx.enter_context(tc.tile_pool(name="stp", bufs=10))
+        tbp = ctx.enter_context(tc.tile_pool(name="tbp", bufs=6))
+        psum_t = ctx.enter_context(tc.psum_pool(name="psum_t", bufs=TP_BUFS))
+        psum_a = ctx.enter_context(tc.psum_pool(name="psum_a", bufs=ACC_BUFS))
+        if MANUAL:
+            ctx.enter_context(tc.manual_schedule())
+
+        sc = const.tile([P, 2, 4], F32, name="sc")
+        wbytes = const.tile([P, NG, 2048], U8, name="wbytes")
+        x_sb = const.tile([P, B, 2048], BF16, name="x_sb")
+
+        def load_w(s):
+            gi = SEQ[s]
+            nc.sync.dma_start(
+                out=wbytes[:, gi, :],
+                in_=W_bytes[256 * gi : 256 * (gi + 1), :].rearrange("(p a) k -> p (a k)", a=2),
+            )
+
+        def load_x(b):
+            nc.sync.dma_start(out=x_sb[:, b, :], in_=x[b].rearrange("(p j) k -> p (j k)", j=2))
+
+        load_w(0)
+        nc.sync.dma_start(out=sc[:], in_=W_scale.rearrange("o (g p t) -> p (o g) t", g=2, p=P, t=4))
+        load_x(0)
+        load_x(1)
+        load_w(1)
+        load_x(2)
+        load_x(3)
+        for s in range(2, NG):
+            load_w(s)
+
+        posi = const.tile([P, 2], I32, name="posi")
+        nc.gpsimd.iota(posi[:], pattern=[[1, 2]], base=0, channel_multiplier=2)
+        ident = const.tile([P, P], F32, name="ident")
+        masks.make_identity(nc, ident[:])
+        zero = const.tile([P, 1], F32, name="zero")
+        nc.vector.memset(zero[:], 0.0)
+        warm = const.tile([P, 1], F32, name="warm")
+        nc.scalar.activation(out=warm[:], in_=zero[:], func=ACTF.Sin)
+
+        ang = const.tile([P, 2, 32], F32, name="ang")
+        nc.vector.tensor_copy(out=ang[:, :, 0:1], in_=posi[:].unsqueeze(2))
+        for w in (1, 2, 4, 8, 16):
+            nc.vector.tensor_scalar(
+                out=ang[:, :, w : 2 * w], in0=ang[:, :, 0:w], scalar1=THETA ** (-2.0 * w / DH), scalar2=None, op0=ALU.mult
+            )
+        angf = ang[:].rearrange("p j i -> p (j i)")
+        ki = const.tile([P, 64], I32, name="ki")
+        nc.vector.tensor_scalar(out=ki[:], in0=angf, scalar1=1.0 / TWO_PI, scalar2=None, op0=ALU.mult)
+        kf = const.tile([P, 64], F32, name="kf")
+        nc.vector.tensor_copy(out=kf[:], in_=ki[:])
+        r1 = const.tile([P, 64], F32, name="r1")
+        nc.vector.scalar_tensor_tensor(out=r1[:], in0=kf[:], scalar=-C1, in1=angf, op0=ALU.mult, op1=ALU.add)
+        r2 = const.tile([P, 64], F32, name="r2")
+        nc.vector.scalar_tensor_tensor(out=r2[:], in0=kf[:], scalar=-C2, in1=r1[:], op0=ALU.mult, op1=ALU.add)
+        r3 = const.tile([P, 64], F32, name="r3")
+        nc.vector.scalar_tensor_tensor(out=r3[:], in0=kf[:], scalar=-C3, in1=r2[:], op0=ALU.mult, op1=ALU.add)
+        qc = const.tile([P, 64], F32, name="qc")
+        nc.vector.tensor_scalar(out=qc[:], in0=r3[:], scalar1=0.25, scalar2=0.5 * math.pi, op0=ALU.mult, op1=ALU.add)
+        s4 = const.tile([P, 64], F32, name="s4")
+        nc.scalar.activation(out=s4[:], in_=r3[:], func=ACTF.Sin, scale=0.25)
+        c4 = const.tile([P, 64], F32, name="c4")
+        nc.scalar.activation(out=c4[:], in_=qc[:], func=ACTF.Sin)
+        ssgn = const.tile([P, 2, 32, 2], F32, name="ssgn")
+        cdup = const.tile([P, 2, 32, 2], F32, name="cdup")
+        cdup64 = cdup[:].rearrange("p j i e -> p j (i e)")
+        sc2 = const.tile([P, 2, 2, 4], F32, name="sc2")
+        sh = const.tile([P, 64], F32, name="sh")
+        nc.gpsimd.tensor_tensor(out=sh[:], in0=s4[:], in1=c4[:], op=ALU.mult)
+        q2 = const.tile([P, 64], F32, name="q2")
+        nc.gpsimd.tensor_tensor(out=q2[:], in0=s4[:], in1=s4[:], op=ALU.mult)
+        c2 = const.tile([P, 64], F32, name="c2")
+        nc.gpsimd.tensor_scalar(out=c2[:], in0=q2[:], scalar1=-2.0, scalar2=1.0, op0=ALU.mult, op1=ALU.add)
+        sq = const.tile([P, 2, 32], F32, name="sq")
+        nc.gpsimd.tensor_tensor(out=sq[:].rearrange("p j i -> p (j i)"), in0=sh[:], in1=c2[:], op=ALU.mult)
+        nc.gpsimd.tensor_scalar(
+            out=ssgn[:, :, :, 0:1], in0=sq[:].unsqueeze(3), scalar1=-4.0, scalar2=0.0, op0=ALU.mult, op1=ALU.add
+        )
+        nc.gpsimd.tensor_scalar(
+            out=ssgn[:, :, :, 1:2], in0=sq[:].unsqueeze(3), scalar1=4.0, scalar2=0.0, op0=ALU.mult, op1=ALU.add
+        )
+        q1 = const.tile([P, 2, 32], F32, name="q1")
+        nc.gpsimd.tensor_tensor(out=q1[:].rearrange("p j i -> p (j i)"), in0=sh[:], in1=sh[:], op=ALU.mult)
+        nc.gpsimd.tensor_scalar(
+            out=cdup[:],
+            in0=q1[:].unsqueeze(3).to_broadcast([P, 2, 32, 2]),
+            scalar1=-8.0,
+            scalar2=1.0,
+            op0=ALU.mult,
+            op1=ALU.add,
+        )
+
+        xg = const.tile([P, B, 2, 1024], BF16, name="xg", align_bytes=64)
+        xc = const.tile([P, B, 512], U32, name="xc", align_bytes=64)
+        xs = const.tile([P, B, 512], U8, name="xs", align_bytes=64)
+
+        def x_turn(b, j, eng):
+            tp = psum_t.tile([P, 512], F32, name="tp")
+            xw = x_sb[:, b, 1024 * j : 1024 * (j + 1)].bitcast(F32)
+            for g in range(2):
+                for u in range(2):
+                    sl = 2 * g + u
+                    nc.tensor.transpose(
+                        tp[:, 128 * sl : 128 * (sl + 1)], xw[:, 256 * g + u : 256 * (g + 1) : 2], ident[:]
+                    )
+            dst = xg[:, b, :, 512 * j : 512 * (j + 1)].bitcast(F32).rearrange("p g (r u) -> p g r u", u=2)
+            src = tp[:].rearrange("p (g u r) -> p g r u", g=2, u=2)
+            if eng == 0:
+                nc.vector.tensor_copy(out=dst, in_=src)
+            else:
+                nc.scalar.copy(out=dst, in_=src)
+
+        def x_quant(b, n):
+            nc.vector.quantize_mx(
+                out=xc[:, b : b + n, :].rearrange("p b c -> p (b c)").bitcast(FP8X4),
+                scales=xs[:, b : b + n, :].rearrange("p b c -> p (b c)"),
+                in_=xg[:, b : b + n, :, :].rearrange("p b g c -> p (b g c)"),
+            )
+
+        wbf_of = {}
+        tp_of = {}
+        wg_of = {}
+        wc_of = {}
+
+        def w_cast(s, a):
+            if a == 0:
+                wbf_new = wbfp.tile([P, 2048], BF16, name="wbf")
+                wbf_of[s] = wbf_new
+            wbf = wbf_of[s]
+            src = wbytes[:, SEQ[s], :].bitcast(FP8)
+            lo = 1024 * a
+            if s < SPLIT_CASTS:
+                nc.vector.tensor_copy(out=wbf[:, lo : lo + 512], in_=src[:, lo : lo + 512])
+                nc.scalar.copy(out=wbf[:, lo + 512 : lo + 1024], in_=src[:, lo + 512 : lo + 1024])
+            else:
+                nc.scalar.copy(out=wbf[:, lo : lo + 1024], in_=src[:, lo : lo + 1024])
+
+        def w_turn(s, g):
+            ww = wbf_of[s][:].bitcast(F32)
+            tp = psum_t.tile([P, 512], F32, name="tp")
+            for a in range(2):
+                for u in range(2):
+                    sl = 2 * a + u
+                    lo = 512 * a + 256 * g
+                    nc.tensor.transpose(tp[:, 128 * sl : 128 * (sl + 1)], ww[:, lo + u : lo + 256 : 2], ident[:])
+            tp_of[(s, g)] = tp
+
+        unit_of = {}
+        for un, unit in enumerate(UNITS):
+            for m, s in enumerate(unit):
+                unit_of[s] = (un, m)
+
+        def wg_half(s, g):
+            un, m = unit_of[s]
+            if un not in wg_of:
+                wg = wgp.tile([P, 2, 2, 1024], BF16, name="wg", align_bytes=64)
+                wg_of[un] = wg
+            return wg_of[un][:, m, g, :]
+
+        def w_scale(s, g):
+            nc.vector.tensor_tensor(
+                out=wg_half(s, g).rearrange("p (r q e) -> p r q e", q=4, e=2),
+                in0=tp_of[(s, g)][:].bitcast(BF16).rearrange("p (q r e) -> p r q e", q=4, e=2),
+                in1=sc2[:, g, :, :].rearrange("p a (u e) -> p (a u) e", e=2).unsqueeze(1).to_broadcast([P, 128, 4, 2]),
+                op=ALU.mult,
+            )
+
+        def w_scale_act(s, g, t):
+            src = tp_of[(s, g)][:].bitcast(BF16).rearrange("p (a u r e) -> p u e r a", a=2, u=2, e=2)
+            dst = wg_half(s, g).rearrange("p (r a t) -> p t r a", a=2, t=4)
+            nc.scalar.activation(out=dst[:, t], in_=src[:, t // 2, t % 2], func=ACTF.Copy, scale=sc[:, g, t : t + 1])
+
+        def w_quant(un):
+            n = len(UNITS[un])
+            wc = wcp.tile([P, 2, 512], U32, name="wc", align_bytes=64)
+            ws = wcp.tile([P, 2, 512], U8, name="ws", align_bytes=64)
+            nc.vector.quantize_mx(
+                out=wc[:, 0:n, :].rearrange("p m c -> p (m c)").bitcast(FP8X4),
+                scales=ws[:, 0:n, :].rearrange("p m c -> p (m c)"),
+                in_=wg_of[un][:, 0:n, :, :].rearrange("p m g c -> p (m g c)"),
+            )
+            wc_of[un] = (wc, ws)
+
+        acc_of = {}
+
+        def project(s, b):
+            un, m = unit_of[s]
+            wc, ws = wc_of[un]
+            acc = psum_a.tile([P, 512], F32, name="acc")
+            acc_of[(s, b)] = acc
+            for j in range(2):
+                for g in range(2):
+                    xcols = slice(256 * g + 128 * j, 256 * g + 128 * (j + 1))
+                    wcols = slice(256 * g, 256 * (g + 1))
+                    nc.tensor.matmul_mx(
+                        out=acc[:, 256 * j : 256 * (j + 1)],
+                        lhsT=xc[:, b, xcols].bitcast(FP8X4),
+                        lhsT_scale=xs[:, b, xcols],
+                        rhs=wc[:, m, wcols].bitcast(FP8X4),
+                        rhs_scale=ws[:, m, wcols],
+                        start=(g == 0),
+                        stop=(g == 1),
+                    )
+
+        def finish(s, b, kind):
+            gi = SEQ[s]
+            acc = acc_of[(s, b)]
+            stage = stp.tile([P, 4, 2, 64], F32, name="stage")
+            st_jhd = stage[:].rearrange("p h j d -> p j h d")
+            acc_jhd = acc[:].rearrange("p (j h d) -> p j h d", j=2, h=4)
+            if gi >= 8:
+                nc.scalar.copy(out=st_jhd, in_=acc_jhd)
+            else:
+                tb = tbp.tile([P, 4, 2, 64], F32, name="tb")
+                nc.vector.tensor_tensor(
+                    out=tb[:].rearrange("p h j (i e) -> p j h i e", e=2),
+                    in0=acc[:].rearrange("p (j h i e) -> p j h i e", j=2, h=4, e=2)[:, :, :, :, ::-1],
+                    in1=ssgn[:].unsqueeze(2).to_broadcast([P, 2, 4, 32, 2]),
+                    op=ALU.mult,
+                )
+                if kind == 1:
+                    nc.scalar.copy(out=st_jhd, in_=acc_jhd)
+                    nc.gpsimd.tensor_tensor(
+                        out=stage[:], in0=stage[:], in1=cdup64.unsqueeze(1).to_broadcast([P, 4, 2, 64]), op=ALU.mult
+                    )
+                else:
+                    nc.vector.tensor_tensor(
+                        out=st_jhd, in0=acc_jhd, in1=cdup64.unsqueeze(2).to_broadcast([P, 2, 4, 64]), op=ALU.mult
+                    )
+                st_flat = stage[:].rearrange("p h j d -> p (h j d)")
+                add_eng = nc.vector if kind == 2 else nc.gpsimd
+                add_eng.tensor_tensor(out=st_flat, in0=st_flat, in1=tb[:].rearrange("p h j d -> p (h j d)"), op=ALU.add)
+            h0 = 4 * (gi % 4)
+            nc.sync.dma_start(
+                out=outs[gi // 4][b, h0 : h0 + 4, :, :].rearrange("h (p j) d -> p h (j d)", j=2),
+                in_=stage[:].rearrange("p h j d -> p h (j d)"),
+            )
+
+        rope_banks = [(s, b) for s in range(NG) if SEQ[s] < 8 for b in range(B)]
+        v_banks = [(s, b) for s in range(NG) if SEQ[s] >= 8 for b in range(B)]
+        n_rope = len(rope_banks)
+
+        slices = []
+        scale_at = {}
+        quant_at = {}
+        for un in range(1, len(UNITS)):
+            for s in UNITS[un]:
+                for g in range(2):
+                    scale_at[(s, g)] = len(slices)
+                    if not (g == 1 and s in SCALE_ON_ACT):
+                        slices.append(("scale", s, g))
+            quant_at[un] = len(slices)
+            slices.append(("quant", un, 0))
+        v_at = []
+        for s, b in v_banks:
+            soonest = quant_at[unit_of[s][0]] + 1
+            if len(v_at) >= 2 and v_at[-1] >= n_rope - LEAD_MM:
+                v_at.append(max(soonest, v_at[-2] + 1))
+            elif v_at:
+                v_at.append(max(soonest, v_at[-1] + 1))
+            else:
+                v_at.append(soonest)
+        last = max(n_rope, len(slices), v_at[-1] + 1)
+
+        w_cast(0, 0)
+        w_cast(0, 1)
+        w_turn(0, 0)
+        w_turn(0, 1)
+        x_turn(0, 0, 1)
+        x_turn(0, 1, 1)
+        nc.vector.tensor_copy(out=sc2[:], in_=sc[:].unsqueeze(2).to_broadcast([P, 2, 2, 4]))
+        w_scale(0, 0)
+        w_scale(0, 1)
+        x_turn(1, 0, 1)
+        x_turn(1, 1, 1)
+        w_quant(0)
+        x_quant(0, 1)
+        project(rope_banks[0][0], rope_banks[0][1])
+        first = -2
+        for i in range(first, last):
+            for s in range(1, NG):
+                on_act = s in SCALE_ON_ACT
+                turn_first = min(scale_at[(s, 0)], scale_at[(s, 1)] - (LEAD_P if on_act else 0)) - LEAD_T
+                for a in range(2):
+                    at = turn_first - LEAD_C + a
+                    if at == i or (i == first and at < first):
+                        w_cast(s, a)
+            for s in range(1, NG):
+                on_act = s in SCALE_ON_ACT
+                for g in (1, 0) if on_act else (0, 1):
+                    at = scale_at[(s, g)] - LEAD_T - (LEAD_P if on_act and g == 1 else 0)
+                    if at == i or (i == first and at < first):
+                        w_turn(s, g)
+            if 2 <= i + 4 < B:
+                x_turn(i + 4, 0, 1)
+                x_turn(i + 4, 1, 1)
+            for s in SCALE_ON_ACT:
+                t = i - (scale_at[(s, 1)] - LEAD_P)
+                if 0 <= t < 4:
+                    w_scale_act(s, 1, t)
+            if 0 <= i < n_rope:
+                kind = KIND_END[i - (n_rope - len(KIND_END))] if i >= n_rope - len(KIND_END) else KIND[i % 8]
+                finish(rope_banks[i][0], rope_banks[i][1], kind)
+            if i == 0:
+                x_quant(1, 1)
+                project(rope_banks[1][0], rope_banks[1][1])
+            if i == 1:
+                x_quant(2, 2)
+                project(rope_banks[2][0], rope_banks[2][1])
+            if 0 <= i < len(slices):
+                what, n, g = slices[i]
+                if what == "scale":
+                    w_scale(n, g)
+                else:
+                    w_quant(n)
+            if 3 <= i + LEAD_MM < n_rope:
+                project(rope_banks[i + LEAD_MM][0], rope_banks[i + LEAD_MM][1])
+            for n, at in enumerate(v_at):
+                if at == i:
+                    project(v_banks[n][0], v_banks[n][1])
+                    finish(v_banks[n][0], v_banks[n][1], 0)

@@ -27,6 +27,8 @@ SCALE_ON_ACT = ()
 KIND = (0, 1, 0, 0, 1, 0, 1, 0)
 KIND_END = (0, 0, 2, 2)
 LEAD_MM = 2
+V_ON_ACT_QUEUE = False
+V_TWO = 27
 SPLIT_CASTS = 2
 LEAD_T = 2
 LEAD_C = 3
@@ -234,10 +236,13 @@ def tile_multiheadselfattention_pa_kernel(tc, x, W_bytes, W_scale, out_0, out_1,
 
         acc_of = {}
 
-        def project(s, b):
+        def project(s, b, spare=False):
             un, m = unit_of[s]
             wc, ws = wc_of[un]
-            acc = psum_a.tile([P, 512], F32, name="acc")
+            if spare:
+                acc = psum_t.tile([P, 512], F32, name="tp")
+            else:
+                acc = psum_a.tile([P, 512], F32, name="acc")
             acc_of[(s, b)] = acc
             for j in range(2):
                 for g in range(2):
@@ -282,7 +287,7 @@ def tile_multiheadselfattention_pa_kernel(tc, x, W_bytes, W_scale, out_0, out_1,
                 add_eng = nc.vector if kind == 2 else nc.gpsimd
                 add_eng.tensor_tensor(out=st_flat, in0=st_flat, in1=tb[:].rearrange("p h j d -> p (h j d)"), op=ALU.add)
             h0 = 4 * (gi % 4)
-            nc.sync.dma_start(
+            (nc.scalar if gi >= 8 and V_ON_ACT_QUEUE else nc.sync).dma_start(
                 out=outs[gi // 4][b, h0 : h0 + 4, :, :].rearrange("h (p j) d -> p h (j d)", j=2),
                 in_=stage[:].rearrange("p h j d -> p h (j d)"),
             )
@@ -305,7 +310,7 @@ def tile_multiheadselfattention_pa_kernel(tc, x, W_bytes, W_scale, out_0, out_1,
         v_at = []
         for s, b in v_banks:
             soonest = quant_at[unit_of[s][0]] + 1
-            if len(v_at) >= 2 and v_at[-1] >= n_rope - LEAD_MM:
+            if len(v_at) >= 2 and v_at[-1] >= V_TWO:
                 v_at.append(max(soonest, v_at[-2] + 1))
             elif v_at:
                 v_at.append(max(soonest, v_at[-1] + 1))
@@ -368,5 +373,5 @@ def tile_multiheadselfattention_pa_kernel(tc, x, W_bytes, W_scale, out_0, out_1,
                 project(rope_banks[i + LEAD_MM][0], rope_banks[i + LEAD_MM][1])
             for n, at in enumerate(v_at):
                 if at == i:
-                    project(v_banks[n][0], v_banks[n][1])
+                    project(v_banks[n][0], v_banks[n][1], i >= V_TWO)
                     finish(v_banks[n][0], v_banks[n][1], 0)

@@ -23,12 +23,11 @@ NG = 12
 SEQ = (0, 4, 1, 5, 8, 2, 6, 3, 9, 10, 7, 11)
 UNITS = ((0,), (1,), (2,), (3, 4), (5,), (6, 7), (8, 9), (10,), (11,))
 MANUAL = True
-SCALE_ON_ACT = ()
+SCALE_ON_ACT = (4, 8)
 KIND = (0, 1, 0, 0, 1, 0, 1, 0)
 KIND_END = (0, 0, 2, 2)
 LEAD_MM = 2
 V_ON_ACT_QUEUE = False
-V_TWO = 27
 SPLIT_CASTS = 2
 LEAD_T = 2
 LEAD_C = 3
@@ -307,10 +306,13 @@ def tile_multiheadselfattention_pa_kernel(tc, x, W_bytes, W_scale, out_0, out_1,
                         slices.append(("scale", s, g))
             quant_at[un] = len(slices)
             slices.append(("quant", un, 0))
+        v_two = 1 + max(
+            scale_at[(s, g)] - LEAD_T - (LEAD_P if g == 1 and s in SCALE_ON_ACT else 0) for s in range(1, NG) for g in range(2)
+        )
         v_at = []
         for s, b in v_banks:
             soonest = quant_at[unit_of[s][0]] + 1
-            if len(v_at) >= 2 and v_at[-1] >= V_TWO:
+            if len(v_at) >= 2 and v_at[-1] >= v_two:
                 v_at.append(max(soonest, v_at[-2] + 1))
             elif v_at:
                 v_at.append(max(soonest, v_at[-1] + 1))
@@ -373,5 +375,5 @@ def tile_multiheadselfattention_pa_kernel(tc, x, W_bytes, W_scale, out_0, out_1,
                 project(rope_banks[i + LEAD_MM][0], rope_banks[i + LEAD_MM][1])
             for n, at in enumerate(v_at):
                 if at == i:
-                    project(v_banks[n][0], v_banks[n][1], i >= V_TWO)
+                    project(v_banks[n][0], v_banks[n][1], i >= v_two)
                     finish(v_banks[n][0], v_banks[n][1], 0)

@@ -20,10 +20,10 @@ FLOPS = 2 * B * L * D * 3 * H * DH
 
 P = 128
 NG = 12
-SEQ = (0, 4, 1, 5, 8, 2, 6, 3, 9, 10, 7, 11)
-UNITS = ((0,), (1,), (2,), (3, 4), (5,), (6, 7), (8, 9), (10,), (11,))
+SEQ = (0, 4, 1, 5, 8, 2, 6, 9, 3, 10, 7, 11)
+UNITS = ((0,), (1,), (2,), (3, 4), (5,), (6,), (7,), (8,), (9,), (10,), (11,))
 MANUAL = True
-SCALE_ON_ACT = (4, 8)
+ACT_HALVES = ((4, 1), (7, 1))
 KIND = (0, 1, 0, 0, 1, 0, 1, 0)
 KIND_END = (0, 0, 2, 2)
 LEAD_MM = 2
@@ -296,19 +296,40 @@ def tile_multiheadselfattention_pa_kernel(tc, x, W_bytes, W_scale, out_0, out_1,
         n_rope = len(rope_banks)
 
         slices = []
-        scale_at = {}
-        quant_at = {}
+        half_slice = {}
         for un in range(1, len(UNITS)):
             for s in UNITS[un]:
                 for g in range(2):
-                    scale_at[(s, g)] = len(slices)
-                    if not (g == 1 and s in SCALE_ON_ACT):
+                    half_slice[(s, g)] = len(slices)
+                    if (s, g) not in ACT_HALVES:
                         slices.append(("scale", s, g))
-            quant_at[un] = len(slices)
             slices.append(("quant", un, 0))
-        v_two = 1 + max(
-            scale_at[(s, g)] - LEAD_T - (LEAD_P if g == 1 and s in SCALE_ON_ACT else 0) for s in range(1, NG) for g in range(2)
-        )
+        rope_it = []
+        slice_it = []
+        quant_at = {0: -LEAD_MM}
+        it = 0
+        while len(rope_it) < n_rope or len(slice_it) < len(slices):
+            if len(rope_it) < n_rope:
+                un = unit_of[rope_banks[len(rope_it)][0]][0]
+                if un in quant_at and quant_at[un] + LEAD_MM <= it:
+                    rope_it.append(it)
+            if len(slice_it) < len(slices):
+                if slices[len(slice_it)][0] == "quant":
+                    quant_at[slices[len(slice_it)][1]] = it
+                slice_it.append(it)
+            it += 1
+        scale_at = {}
+        for s in range(NG - 1, 0, -1):
+            for g in (1, 0):
+                if (s, g) in ACT_HALVES:
+                    nxt = (s, 1) if g == 0 else (s + 1, 0)
+                    if nxt in ACT_HALVES and half_slice[nxt] == half_slice[(s, g)]:
+                        scale_at[(s, g)] = scale_at[nxt] - LEAD_P
+                    else:
+                        scale_at[(s, g)] = slice_it[half_slice[(s, g)]] - LEAD_P
+                else:
+                    scale_at[(s, g)] = slice_it[half_slice[(s, g)]]
+        v_two = 1 + max(scale_at[(s, g)] - LEAD_T for s in range(1, NG) for g in range(2))
         v_at = []
         for s, b in v_banks:
             soonest = quant_at[unit_of[s][0]] + 1
@@ -318,7 +339,7 @@ def tile_multiheadselfattention_pa_kernel(tc, x, W_bytes, W_scale, out_0, out_1,
                 v_at.append(max(soonest, v_at[-1] + 1))
             else:
                 v_at.append(soonest)
-        last = max(n_rope, len(slices), v_at[-1] + 1)
+        last = max(it, v_at[-1] + 1)
 
         w_cast(0, 0)
         w_cast(0, 1)
@@ -336,44 +357,53 @@ def tile_multiheadselfattention_pa_kernel(tc, x, W_bytes, W_scale, out_0, out_1,
         project(rope_banks[0][0], rope_banks[0][1])
         first = -2
         for i in range(first, last):
+            if i == first:
+                for s in range(1, NG):
+                    turn_first = min(scale_at[(s, 0)], scale_at[(s, 1)]) - LEAD_T
+                    for a in range(2):
+                        at = turn_first - LEAD_C + a
+                        if at == i or (i == first and at < first):
+                            w_cast(s, a)
             for s in range(1, NG):
-                on_act = s in SCALE_ON_ACT
-                turn_first = min(scale_at[(s, 0)], scale_at[(s, 1)] - (LEAD_P if on_act else 0)) - LEAD_T
-                for a in range(2):
-                    at = turn_first - LEAD_C + a
-                    if at == i or (i == first and at < first):
-                        w_cast(s, a)
-            for s in range(1, NG):
-                on_act = s in SCALE_ON_ACT
-                for g in (1, 0) if on_act else (0, 1):
-                    at = scale_at[(s, g)] - LEAD_T - (LEAD_P if on_act and g == 1 else 0)
+                for g in (0, 1) if scale_at[(s, 0)] <= scale_at[(s, 1)] else (1, 0):
+                    at = scale_at[(s, g)] - LEAD_T
                     if at == i or (i == first and at < first):
                         w_turn(s, g)
             if 2 <= i + 4 < B:
                 x_turn(i + 4, 0, 1)
                 x_turn(i + 4, 1, 1)
-            for s in SCALE_ON_ACT:
-                t = i - (scale_at[(s, 1)] - LEAD_P)
-                if 0 <= t < 4:
-                    w_scale_act(s, 1, t)
-            if 0 <= i < n_rope:
-                kind = KIND_END[i - (n_rope - len(KIND_END))] if i >= n_rope - len(KIND_END) else KIND[i % 8]
-                finish(rope_banks[i][0], rope_banks[i][1], kind)
+            for r in range(n_rope):
+                if rope_it[r] == i:
+                    kind = KIND_END[r - (n_rope - len(KIND_END))] if r >= n_rope - len(KIND_END) else KIND[r % 8]
+                    finish(rope_banks[r][0], rope_banks[r][1], kind)
             if i == 0:
                 x_quant(1, 1)
                 project(rope_banks[1][0], rope_banks[1][1])
             if i == 1:
                 x_quant(2, 2)
                 project(rope_banks[2][0], rope_banks[2][1])
-            if 0 <= i < len(slices):
-                what, n, g = slices[i]
-                if what == "scale":
-                    w_scale(n, g)
-                else:
-                    w_quant(n)
-            if 3 <= i + LEAD_MM < n_rope:
-                project(rope_banks[i + LEAD_MM][0], rope_banks[i + LEAD_MM][1])
+            for k in range(len(slices)):
+                if slice_it[k] == i:
+                    what, n, g = slices[k]
+                    if what == "scale":
+                        w_scale(n, g)
+                    else:
+                        w_quant(n)
+            for r in range(3, n_rope):
+                if rope_it[r] - LEAD_MM == i:
+                    project(rope_banks[r][0], rope_banks[r][1])
             for n, at in enumerate(v_at):
                 if at == i:
                     project(v_banks[n][0], v_banks[n][1], i >= v_two)
                     finish(v_banks[n][0], v_banks[n][1], 0)
+            for s, g in ACT_HALVES:
+                t = i - scale_at[(s, g)]
+                if 0 <= t < 4:
+                    w_scale_act(s, g, t)
+            if i > first:
+                for s in range(1, NG):
+                    turn_first = min(scale_at[(s, 0)], scale_at[(s, 1)]) - LEAD_T
+                    for a in range(2):
+                        at = turn_first - LEAD_C + a
+                        if at == i or (i == first and at < first):
+                            w_cast(s, a)

@@ -21,17 +21,16 @@ FLOPS = 2 * B * L * D * 3 * H * DH
 P = 128
 NG = 12
 SEQ = (0, 4, 1, 5, 8, 2, 6, 9, 3, 10, 7, 11)
-UNITS = ((0,), (1,), (2,), (3, 4), (5,), (6,), (7,), (8,), (9,), (10,), (11,))
+UNITS = ((0,), (1,), (2,), (3, 4), (5,), (6,), (7,), (8, 9), (10,), (11,))
 MANUAL = True
 ACT_HALVES = ((4, 1), (7, 1))
 KIND = (0, 1, 0, 0, 1, 0, 1, 0)
 KIND_END = (0, 0, 2, 2)
 LEAD_MM = 2
-V_ON_ACT_QUEUE = False
 SPLIT_CASTS = 2
-LEAD_T = 2
+LEAD_T = 1
 LEAD_C = 3
-LEAD_P = 4
+LEAD_P = 5
 TP_BUFS = 4
 ACC_BUFS = 4
 
@@ -257,6 +256,16 @@ def tile_multiheadselfattention_pa_kernel(tc, x, W_bytes, W_scale, out_0, out_1,
                         stop=(g == 1),
                     )
 
+        late_stores = []
+
+        def store(s, b, stage):
+            gi = SEQ[s]
+            h0 = 4 * (gi % 4)
+            nc.sync.dma_start(
+                out=outs[gi // 4][b, h0 : h0 + 4, :, :].rearrange("h (p j) d -> p h (j d)", j=2),
+                in_=stage[:].rearrange("p h j d -> p h (j d)"),
+            )
+
         def finish(s, b, kind):
             gi = SEQ[s]
             acc = acc_of[(s, b)]
@@ -285,11 +294,10 @@ def tile_multiheadselfattention_pa_kernel(tc, x, W_bytes, W_scale, out_0, out_1,
                 st_flat = stage[:].rearrange("p h j d -> p (h j d)")
                 add_eng = nc.vector if kind == 2 else nc.gpsimd
                 add_eng.tensor_tensor(out=st_flat, in0=st_flat, in1=tb[:].rearrange("p h j d -> p (h j d)"), op=ALU.add)
-            h0 = 4 * (gi % 4)
-            (nc.scalar if gi >= 8 and V_ON_ACT_QUEUE else nc.sync).dma_start(
-                out=outs[gi // 4][b, h0 : h0 + 4, :, :].rearrange("h (p j) d -> p h (j d)", j=2),
-                in_=stage[:].rearrange("p h j d -> p h (j d)"),
-            )
+            if gi >= 8:
+                store(s, b, stage)
+            else:
+                late_stores.append((s, b, stage))
 
         rope_banks = [(s, b) for s in range(NG) if SEQ[s] < 8 for b in range(B)]
         v_banks = [(s, b) for s in range(NG) if SEQ[s] >= 8 for b in range(B)]
@@ -396,6 +404,9 @@ def tile_multiheadselfattention_pa_kernel(tc, x, W_bytes, W_scale, out_0, out_1,
                 if at == i:
                     project(v_banks[n][0], v_banks[n][1], i >= v_two)
                     finish(v_banks[n][0], v_banks[n][1], 0)
+            for u in late_stores:
+                store(u[0], u[1], u[2])
+            late_stores.clear()
             for s, g in ACT_HALVES:
                 t = i - scale_at[(s, g)]
                 if 0 <= t < 4:

@@ -21,16 +21,18 @@ FLOPS = 2 * B * L * D * 3 * H * DH
 P = 128
 NG = 12
 SEQ = (0, 4, 1, 5, 8, 2, 6, 9, 3, 10, 7, 11)
-UNITS = ((0,), (1,), (2,), (3, 4), (5,), (6,), (7,), (8, 9), (10,), (11,))
-MANUAL = True
-ACT_HALVES = ((4, 1), (7, 1))
-KIND = (0, 1, 0, 0, 1, 0, 1, 0)
-KIND_END = (0, 0, 2, 2)
+S_HALF = (3, 4, 5, 6, 7, 8, 9, 10, 11)
+G_WEAVE = ()
+Q0 = 2
+QNUM = 5
+QDEN = 2
 LEAD_MM = 2
-SPLIT_CASTS = 2
 LEAD_T = 1
 LEAD_C = 3
-LEAD_P = 5
+LEAD_W = 3
+LEAD_PL = 1
+N_VADD = 2
+SPLIT_CASTS = 2
 TP_BUFS = 4
 ACC_BUFS = 4
 
@@ -46,15 +48,15 @@ def tile_multiheadselfattention_pa_kernel(tc, x, W_bytes, W_scale, out_0, out_1,
 
     with ExitStack() as ctx:
         const = ctx.enter_context(tc.tile_pool(name="const", bufs=1))
-        wbfp = ctx.enter_context(tc.tile_pool(name="wbfp", bufs=4))
-        wgp = ctx.enter_context(tc.tile_pool(name="wgp", bufs=2))
-        wcp = ctx.enter_context(tc.tile_pool(name="wcp", bufs=3))
+        wbfp = ctx.enter_context(tc.tile_pool(name="wbfp", bufs=7))
+        wgp = ctx.enter_context(tc.tile_pool(name="wgp", bufs=6))
+        wcp = ctx.enter_context(tc.tile_pool(name="wcp", bufs=4))
         stp = ctx.enter_context(tc.tile_pool(name="stp", bufs=10))
         tbp = ctx.enter_context(tc.tile_pool(name="tbp", bufs=6))
+        plp = ctx.enter_context(tc.tile_pool(name="plp", bufs=4))
         psum_t = ctx.enter_context(tc.psum_pool(name="psum_t", bufs=TP_BUFS))
         psum_a = ctx.enter_context(tc.psum_pool(name="psum_a", bufs=ACC_BUFS))
-        if MANUAL:
-            ctx.enter_context(tc.manual_schedule())
+        ctx.enter_context(tc.manual_schedule())
 
         sc = const.tile([P, 2, 4], F32, name="sc")
         wbytes = const.tile([P, NG, 2048], U8, name="wbytes")
@@ -172,6 +174,7 @@ def tile_multiheadselfattention_pa_kernel(tc, x, W_bytes, W_scale, out_0, out_1,
         tp_of = {}
         wg_of = {}
         wc_of = {}
+        pl_of = {}
 
         def w_cast(s, a):
             if a == 0:
@@ -196,17 +199,11 @@ def tile_multiheadselfattention_pa_kernel(tc, x, W_bytes, W_scale, out_0, out_1,
                     nc.tensor.transpose(tp[:, 128 * sl : 128 * (sl + 1)], ww[:, lo + u : lo + 256 : 2], ident[:])
             tp_of[(s, g)] = tp
 
-        unit_of = {}
-        for un, unit in enumerate(UNITS):
-            for m, s in enumerate(unit):
-                unit_of[s] = (un, m)
-
         def wg_half(s, g):
-            un, m = unit_of[s]
-            if un not in wg_of:
-                wg = wgp.tile([P, 2, 2, 1024], BF16, name="wg", align_bytes=64)
-                wg_of[un] = wg
-            return wg_of[un][:, m, g, :]
+            if s not in wg_of:
+                wg = wgp.tile([P, 2, 1024], BF16, name="wg", align_bytes=64)
+                wg_of[s] = wg
+            return wg_of[s][:, g, :]
 
         def w_scale(s, g):
             nc.vector.tensor_tensor(
@@ -216,27 +213,36 @@ def tile_multiheadselfattention_pa_kernel(tc, x, W_bytes, W_scale, out_0, out_1,
                 op=ALU.mult,
             )
 
-        def w_scale_act(s, g, t):
+        def w_plane(s, g, t):
+            if t == 0:
+                pl = plp.tile([P, 4, 256], BF16, name="pl")
+                pl_of[(s, g)] = pl
             src = tp_of[(s, g)][:].bitcast(BF16).rearrange("p (a u r e) -> p u e r a", a=2, u=2, e=2)
-            dst = wg_half(s, g).rearrange("p (r a t) -> p t r a", a=2, t=4)
-            nc.scalar.activation(out=dst[:, t], in_=src[:, t // 2, t % 2], func=ACTF.Copy, scale=sc[:, g, t : t + 1])
+            dst = pl_of[(s, g)][:, t, :].rearrange("p (r a) -> p r a", a=2)
+            nc.scalar.activation(out=dst, in_=src[:, t // 2, t % 2], func=ACTF.Copy, scale=sc[:, g, t : t + 1])
 
-        def w_quant(un):
-            n = len(UNITS[un])
-            wc = wcp.tile([P, 2, 512], U32, name="wc", align_bytes=64)
-            ws = wcp.tile([P, 2, 512], U8, name="ws", align_bytes=64)
+        def w_weave(s, g):
+            dst = wg_half(s, g).rearrange("p (c t) -> p c t", t=4)
+            src = pl_of[(s, g)][:].rearrange("p t c -> p c t")
+            if s in G_WEAVE:
+                nc.gpsimd.tensor_scalar(out=dst, in0=src, scalar1=1.0, scalar2=0.0, op0=ALU.mult, op1=ALU.add)
+            else:
+                nc.scalar.copy(out=dst, in_=src)
+
+        def w_quant(s):
+            wc = wcp.tile([P, 512], U32, name="wc", align_bytes=64)
+            ws = wcp.tile([P, 512], U8, name="ws", align_bytes=64)
             nc.vector.quantize_mx(
-                out=wc[:, 0:n, :].rearrange("p m c -> p (m c)").bitcast(FP8X4),
-                scales=ws[:, 0:n, :].rearrange("p m c -> p (m c)"),
-                in_=wg_of[un][:, 0:n, :, :].rearrange("p m g c -> p (m g c)"),
+                out=wc[:].bitcast(FP8X4), scales=ws[:], in_=wg_of[s][:].rearrange("p g c -> p (g c)")
             )
-            wc_of[un] = (wc, ws)
+            wc_of[s] = (wc, ws)
 
         acc_of = {}
+        st_of = {}
+        tb_of = {}
 
         def project(s, b, spare=False):
-            un, m = unit_of[s]
-            wc, ws = wc_of[un]
+            wc, ws = wc_of[s]
             if spare:
                 acc = psum_t.tile([P, 512], F32, name="tp")
             else:
@@ -250,104 +256,92 @@ def tile_multiheadselfattention_pa_kernel(tc, x, W_bytes, W_scale, out_0, out_1,
                         out=acc[:, 256 * j : 256 * (j + 1)],
                         lhsT=xc[:, b, xcols].bitcast(FP8X4),
                         lhsT_scale=xs[:, b, xcols],
-                        rhs=wc[:, m, wcols].bitcast(FP8X4),
-                        rhs_scale=ws[:, m, wcols],
+                        rhs=wc[:, wcols].bitcast(FP8X4),
+                        rhs_scale=ws[:, wcols],
                         start=(g == 0),
                         stop=(g == 1),
                     )
 
-        late_stores = []
-
-        def store(s, b, stage):
+        def store(s, b):
             gi = SEQ[s]
             h0 = 4 * (gi % 4)
             nc.sync.dma_start(
                 out=outs[gi // 4][b, h0 : h0 + 4, :, :].rearrange("h (p j) d -> p h (j d)", j=2),
-                in_=stage[:].rearrange("p h j d -> p h (j d)"),
+                in_=st_of[(s, b)][:].rearrange("p h j d -> p h (j d)"),
             )
 
-        def finish(s, b, kind):
-            gi = SEQ[s]
-            acc = acc_of[(s, b)]
+        def v_out(s, b):
             stage = stp.tile([P, 4, 2, 64], F32, name="stage")
-            st_jhd = stage[:].rearrange("p h j d -> p j h d")
-            acc_jhd = acc[:].rearrange("p (j h d) -> p j h d", j=2, h=4)
-            if gi >= 8:
-                nc.scalar.copy(out=st_jhd, in_=acc_jhd)
-            else:
-                tb = tbp.tile([P, 4, 2, 64], F32, name="tb")
-                nc.vector.tensor_tensor(
-                    out=tb[:].rearrange("p h j (i e) -> p j h i e", e=2),
-                    in0=acc[:].rearrange("p (j h i e) -> p j h i e", j=2, h=4, e=2)[:, :, :, :, ::-1],
-                    in1=ssgn[:].unsqueeze(2).to_broadcast([P, 2, 4, 32, 2]),
-                    op=ALU.mult,
-                )
-                if kind == 1:
-                    nc.scalar.copy(out=st_jhd, in_=acc_jhd)
-                    nc.gpsimd.tensor_tensor(
-                        out=stage[:], in0=stage[:], in1=cdup64.unsqueeze(1).to_broadcast([P, 4, 2, 64]), op=ALU.mult
-                    )
-                else:
-                    nc.vector.tensor_tensor(
-                        out=st_jhd, in0=acc_jhd, in1=cdup64.unsqueeze(2).to_broadcast([P, 2, 4, 64]), op=ALU.mult
-                    )
-                st_flat = stage[:].rearrange("p h j d -> p (h j d)")
-                add_eng = nc.vector if kind == 2 else nc.gpsimd
-                add_eng.tensor_tensor(out=st_flat, in0=st_flat, in1=tb[:].rearrange("p h j d -> p (h j d)"), op=ALU.add)
-            if gi >= 8:
-                store(s, b, stage)
-            else:
-                late_stores.append((s, b, stage))
+            st_of[(s, b)] = stage
+            nc.scalar.copy(
+                out=stage[:].rearrange("p h j d -> p j h d"),
+                in_=acc_of[(s, b)][:].rearrange("p (j h d) -> p j h d", j=2, h=4),
+            )
+
+        def rope_sin(s, b):
+            tb = tbp.tile([P, 4, 2, 64], F32, name="tb")
+            tb_of[(s, b)] = tb
+            nc.vector.tensor_tensor(
+                out=tb[:].rearrange("p h j (i e) -> p j h i e", e=2),
+                in0=acc_of[(s, b)][:].rearrange("p (j h i e) -> p j h i e", j=2, h=4, e=2)[:, :, :, :, ::-1],
+                in1=ssgn[:].unsqueeze(2).to_broadcast([P, 2, 4, 32, 2]),
+                op=ALU.mult,
+            )
+
+        def rope_cos(s, b):
+            stage = stp.tile([P, 4, 2, 64], F32, name="stage")
+            st_of[(s, b)] = stage
+            nc.vector.tensor_tensor(
+                out=stage[:].rearrange("p h j d -> p j h d"),
+                in0=acc_of[(s, b)][:].rearrange("p (j h d) -> p j h d", j=2, h=4),
+                in1=cdup64.unsqueeze(2).to_broadcast([P, 2, 4, 64]),
+                op=ALU.mult,
+            )
+
+        def rope_add(s, b, eng):
+            st_flat = st_of[(s, b)][:].rearrange("p h j d -> p (h j d)")
+            eng.tensor_tensor(out=st_flat, in0=st_flat, in1=tb_of[(s, b)][:].rearrange("p h j d -> p (h j d)"), op=ALU.add)
 
         rope_banks = [(s, b) for s in range(NG) if SEQ[s] < 8 for b in range(B)]
         v_banks = [(s, b) for s in range(NG) if SEQ[s] >= 8 for b in range(B)]
         n_rope = len(rope_banks)
-
-        slices = []
-        half_slice = {}
-        for un in range(1, len(UNITS)):
-            for s in UNITS[un]:
-                for g in range(2):
-                    half_slice[(s, g)] = len(slices)
-                    if (s, g) not in ACT_HALVES:
-                        slices.append(("scale", s, g))
-            slices.append(("quant", un, 0))
-        rope_it = []
-        slice_it = []
-        quant_at = {0: -LEAD_MM}
-        it = 0
-        while len(rope_it) < n_rope or len(slice_it) < len(slices):
-            if len(rope_it) < n_rope:
-                un = unit_of[rope_banks[len(rope_it)][0]][0]
-                if un in quant_at and quant_at[un] + LEAD_MM <= it:
-                    rope_it.append(it)
-            if len(slice_it) < len(slices):
-                if slices[len(slice_it)][0] == "quant":
-                    quant_at[slices[len(slice_it)][1]] = it
-                slice_it.append(it)
-            it += 1
+        quant_at = {s: Q0 + (s - 1) * QNUM // QDEN for s in range(1, NG)}
+        for r in range(B, n_rope):
+            assert quant_at[rope_banks[r][0]] + LEAD_MM <= r
         scale_at = {}
-        for s in range(NG - 1, 0, -1):
-            for g in (1, 0):
-                if (s, g) in ACT_HALVES:
-                    nxt = (s, 1) if g == 0 else (s + 1, 0)
-                    if nxt in ACT_HALVES and half_slice[nxt] == half_slice[(s, g)]:
-                        scale_at[(s, g)] = scale_at[nxt] - LEAD_P
-                    else:
-                        scale_at[(s, g)] = slice_it[half_slice[(s, g)]] - LEAD_P
-                else:
-                    scale_at[(s, g)] = slice_it[half_slice[(s, g)]]
-        v_two = 1 + max(scale_at[(s, g)] - LEAD_T for s in range(1, NG) for g in range(2))
+        plane_at = {}
+        weave_at = {}
+        turn_at = {}
+        for s in range(1, NG):
+            if s in S_HALF:
+                scale_at[(s, 0)] = quant_at[s] - 1
+                weave_at[s] = quant_at[s] - LEAD_W
+                plane_at[s] = weave_at[s] - LEAD_PL
+                turn_at[(s, 1)] = plane_at[s] - LEAD_T
+            else:
+                scale_at[(s, 0)] = quant_at[s] - 2
+                scale_at[(s, 1)] = quant_at[s] - 1
+                turn_at[(s, 1)] = scale_at[(s, 1)] - LEAD_T
+            turn_at[(s, 0)] = scale_at[(s, 0)] - LEAD_T
+        cast_at = {}
+        for s in range(1, NG):
+            for a in range(2):
+                cast_at[(s, a)] = min(turn_at[(s, 0)], turn_at[(s, 1)]) - LEAD_C + a
+        v_two = 1 + max(turn_at.values())
         v_at = []
         for s, b in v_banks:
-            soonest = quant_at[unit_of[s][0]] + 1
+            soonest = quant_at[s] + 1
             if len(v_at) >= 2 and v_at[-1] >= v_two:
                 v_at.append(max(soonest, v_at[-2] + 1))
             elif v_at:
                 v_at.append(max(soonest, v_at[-1] + 1))
             else:
                 v_at.append(soonest)
-        last = max(it, v_at[-1] + 1)
+        last = max(n_rope, v_at[-1] + 1)
+        first = -2
+
+        def due(at, i):
+            return at == i or (i == first and at < first)
 
         w_cast(0, 0)
         w_cast(0, 1)
@@ -363,58 +357,55 @@ def tile_multiheadselfattention_pa_kernel(tc, x, W_bytes, W_scale, out_0, out_1,
         w_quant(0)
         x_quant(0, 1)
         project(rope_banks[0][0], rope_banks[0][1])
-        first = -2
         for i in range(first, last):
             if i == first:
                 for s in range(1, NG):
-                    turn_first = min(scale_at[(s, 0)], scale_at[(s, 1)]) - LEAD_T
                     for a in range(2):
-                        at = turn_first - LEAD_C + a
-                        if at == i or (i == first and at < first):
+                        if cast_at[(s, a)] < first:
                             w_cast(s, a)
             for s in range(1, NG):
-                for g in (0, 1) if scale_at[(s, 0)] <= scale_at[(s, 1)] else (1, 0):
-                    at = scale_at[(s, g)] - LEAD_T
-                    if at == i or (i == first and at < first):
+                for g in (1, 0) if s in S_HALF else (0, 1):
+                    if due(turn_at[(s, g)], i):
                         w_turn(s, g)
-            if 2 <= i + 4 < B:
-                x_turn(i + 4, 0, 1)
-                x_turn(i + 4, 1, 1)
-            for r in range(n_rope):
-                if rope_it[r] == i:
-                    kind = KIND_END[r - (n_rope - len(KIND_END))] if r >= n_rope - len(KIND_END) else KIND[r % 8]
-                    finish(rope_banks[r][0], rope_banks[r][1], kind)
+            if i == -1:
+                x_turn(2, 0, 1)
+                x_turn(2, 1, 1)
+            if 0 <= i < n_rope:
+                s, b = rope_banks[i]
+                rope_sin(s, b)
+                if i + 1 < B:
+                    x_quant(i + 1, 1)
+                for q in range(1, NG):
+                    if quant_at[q] == i:
+                        w_quant(q)
+                rope_cos(s, b)
+                rope_add(s, b, nc.vector if i >= n_rope - N_VADD else nc.gpsimd)
+            if 0 <= i and i + 1 < B:
+                project(rope_banks[i + 1][0], rope_banks[i + 1][1])
+            for s in range(1, NG):
+                for g in range(2):
+                    if (s, g) in scale_at and scale_at[(s, g)] == i:
+                        w_scale(s, g)
             if i == 0:
-                x_quant(1, 1)
-                project(rope_banks[1][0], rope_banks[1][1])
-            if i == 1:
-                x_quant(2, 2)
-                project(rope_banks[2][0], rope_banks[2][1])
-            for k in range(len(slices)):
-                if slice_it[k] == i:
-                    what, n, g = slices[k]
-                    if what == "scale":
-                        w_scale(n, g)
-                    else:
-                        w_quant(n)
-            for r in range(3, n_rope):
-                if rope_it[r] - LEAD_MM == i:
-                    project(rope_banks[r][0], rope_banks[r][1])
+                x_turn(3, 0, 1)
+                x_turn(3, 1, 1)
+            if 2 <= i and i + LEAD_MM < n_rope:
+                project(rope_banks[i + LEAD_MM][0], rope_banks[i + LEAD_MM][1])
             for n, at in enumerate(v_at):
                 if at == i:
                     project(v_banks[n][0], v_banks[n][1], i >= v_two)
-                    finish(v_banks[n][0], v_banks[n][1], 0)
-            for u in late_stores:
-                store(u[0], u[1], u[2])
-            late_stores.clear()
-            for s, g in ACT_HALVES:
-                t = i - scale_at[(s, g)]
-                if 0 <= t < 4:
-                    w_scale_act(s, g, t)
-            if i > first:
-                for s in range(1, NG):
-                    turn_first = min(scale_at[(s, 0)], scale_at[(s, 1)]) - LEAD_T
-                    for a in range(2):
-                        at = turn_first - LEAD_C + a
-                        if at == i or (i == first and at < first):
-                            w_cast(s, a)
+                    v_out(v_banks[n][0], v_banks[n][1])
+                    store(v_banks[n][0], v_banks[n][1])
+            if 0 <= i < n_rope:
+                store(rope_banks[i][0], rope_banks[i][1])
+            for s in S_HALF:
+                if due(plane_at[s], i):
+                    for t in range(4):
+                        w_plane(s, 1, t)
+            for s in S_HALF:
+                if due(weave_at[s], i):
+                    w_weave(s, 1)
+            for s in range(1, NG):
+                for a in range(2):
+                    if cast_at[(s, a)] == i:
+                        w_cast(s, a)

@@ -31,7 +31,7 @@ LEAD_T = 1
 LEAD_C = 3
 LEAD_W = 3
 LEAD_PL = 1
-N_VADD = 2
+V_ADDS = (31,)
 SPLIT_CASTS = 2
 TP_BUFS = 4
 ACC_BUFS = 4
@@ -72,7 +72,11 @@ def tile_multiheadselfattention_pa_kernel(tc, x, W_bytes, W_scale, out_0, out_1,
         def load_x(b):
             nc.sync.dma_start(out=x_sb[:, b, :], in_=x[b].rearrange("(p j) k -> p (j k)", j=2))
 
-        load_w(0)
+        for g in range(2):
+            nc.sync.dma_start(
+                out=wbytes[:, SEQ[0], :].rearrange("p (a k) -> p a k", a=2)[:, :, 512 * g : 512 * (g + 1)],
+                in_=W_bytes[256 * SEQ[0] : 256 * (SEQ[0] + 1), 512 * g : 512 * (g + 1)].rearrange("(p a) k -> p a k", a=2),
+            )
         nc.sync.dma_start(out=sc[:], in_=W_scale.rearrange("o (g p t) -> p (o g) t", g=2, p=P, t=4))
         load_x(0)
         load_x(1)
@@ -379,7 +383,7 @@ def tile_multiheadselfattention_pa_kernel(tc, x, W_bytes, W_scale, out_0, out_1,
                     if quant_at[q] == i:
                         w_quant(q)
                 rope_cos(s, b)
-                rope_add(s, b, nc.vector if i >= n_rope - N_VADD else nc.gpsimd)
+                rope_add(s, b, nc.vector if i in V_ADDS else nc.gpsimd)
             if 0 <= i and i + 1 < B:
                 project(rope_banks[i + 1][0], rope_banks[i + 1][1])
             for s in range(1, NG):

@@ -111,41 +111,43 @@ def tile_multiheadselfattention_pa_kernel(tc, x, W_bytes, W_scale, out_0, out_1,
         r2 = const.tile([P, 64], F32, name="r2")
         nc.vector.scalar_tensor_tensor(out=r2[:], in0=kf[:], scalar=-C2, in1=r1[:], op0=ALU.mult, op1=ALU.add)
         r3 = const.tile([P, 64], F32, name="r3")
-        nc.vector.scalar_tensor_tensor(out=r3[:], in0=kf[:], scalar=-C3, in1=r2[:], op0=ALU.mult, op1=ALU.add)
         qc = const.tile([P, 64], F32, name="qc")
-        nc.vector.tensor_scalar(out=qc[:], in0=r3[:], scalar1=0.25, scalar2=0.5 * math.pi, op0=ALU.mult, op1=ALU.add)
         s4 = const.tile([P, 64], F32, name="s4")
-        nc.scalar.activation(out=s4[:], in_=r3[:], func=ACTF.Sin, scale=0.25)
         c4 = const.tile([P, 64], F32, name="c4")
-        nc.scalar.activation(out=c4[:], in_=qc[:], func=ACTF.Sin)
         ssgn = const.tile([P, 2, 32, 2], F32, name="ssgn")
         cdup = const.tile([P, 2, 32, 2], F32, name="cdup")
         cdup64 = cdup[:].rearrange("p j i e -> p j (i e)")
         sc2 = const.tile([P, 2, 2, 4], F32, name="sc2")
         sh = const.tile([P, 64], F32, name="sh")
-        nc.gpsimd.tensor_tensor(out=sh[:], in0=s4[:], in1=c4[:], op=ALU.mult)
         q2 = const.tile([P, 64], F32, name="q2")
-        nc.gpsimd.tensor_tensor(out=q2[:], in0=s4[:], in1=s4[:], op=ALU.mult)
         c2 = const.tile([P, 64], F32, name="c2")
-        nc.gpsimd.tensor_scalar(out=c2[:], in0=q2[:], scalar1=-2.0, scalar2=1.0, op0=ALU.mult, op1=ALU.add)
         sq = const.tile([P, 2, 32], F32, name="sq")
-        nc.gpsimd.tensor_tensor(out=sq[:].rearrange("p j i -> p (j i)"), in0=sh[:], in1=c2[:], op=ALU.mult)
-        nc.gpsimd.tensor_scalar(
-            out=ssgn[:, :, :, 0:1], in0=sq[:].unsqueeze(3), scalar1=-4.0, scalar2=0.0, op0=ALU.mult, op1=ALU.add
-        )
-        nc.gpsimd.tensor_scalar(
-            out=ssgn[:, :, :, 1:2], in0=sq[:].unsqueeze(3), scalar1=4.0, scalar2=0.0, op0=ALU.mult, op1=ALU.add
-        )
         q1 = const.tile([P, 2, 32], F32, name="q1")
-        nc.gpsimd.tensor_tensor(out=q1[:].rearrange("p j i -> p (j i)"), in0=sh[:], in1=sh[:], op=ALU.mult)
-        nc.gpsimd.tensor_scalar(
-            out=cdup[:],
-            in0=q1[:].unsqueeze(3).to_broadcast([P, 2, 32, 2]),
-            scalar1=-8.0,
-            scalar2=1.0,
-            op0=ALU.mult,
-            op1=ALU.add,
-        )
+
+        def end_tables():
+            nc.vector.scalar_tensor_tensor(out=r3[:], in0=kf[:], scalar=-C3, in1=r2[:], op0=ALU.mult, op1=ALU.add)
+            nc.vector.tensor_scalar(out=qc[:], in0=r3[:], scalar1=0.25, scalar2=0.5 * math.pi, op0=ALU.mult, op1=ALU.add)
+            nc.scalar.activation(out=s4[:], in_=r3[:], func=ACTF.Sin, scale=0.25)
+            nc.scalar.activation(out=c4[:], in_=qc[:], func=ACTF.Sin)
+            nc.gpsimd.tensor_tensor(out=sh[:], in0=s4[:], in1=c4[:], op=ALU.mult)
+            nc.gpsimd.tensor_tensor(out=q2[:], in0=s4[:], in1=s4[:], op=ALU.mult)
+            nc.gpsimd.tensor_scalar(out=c2[:], in0=q2[:], scalar1=-2.0, scalar2=1.0, op0=ALU.mult, op1=ALU.add)
+            nc.gpsimd.tensor_tensor(out=sq[:].rearrange("p j i -> p (j i)"), in0=sh[:], in1=c2[:], op=ALU.mult)
+            nc.gpsimd.tensor_scalar(
+                out=ssgn[:, :, :, 0:1], in0=sq[:].unsqueeze(3), scalar1=-4.0, scalar2=0.0, op0=ALU.mult, op1=ALU.add
+            )
+            nc.gpsimd.tensor_scalar(
+                out=ssgn[:, :, :, 1:2], in0=sq[:].unsqueeze(3), scalar1=4.0, scalar2=0.0, op0=ALU.mult, op1=ALU.add
+            )
+            nc.gpsimd.tensor_tensor(out=q1[:].rearrange("p j i -> p (j i)"), in0=sh[:], in1=sh[:], op=ALU.mult)
+            nc.gpsimd.tensor_scalar(
+                out=cdup[:],
+                in0=q1[:].unsqueeze(3).to_broadcast([P, 2, 32, 2]),
+                scalar1=-8.0,
+                scalar2=1.0,
+                op0=ALU.mult,
+                op1=ALU.add,
+            )
 
         xg = const.tile([P, B, 2, 1024], BF16, name="xg", align_bytes=64)
         xc = const.tile([P, B, 512], U32, name="xc", align_bytes=64)
@@ -349,6 +351,7 @@ def tile_multiheadselfattention_pa_kernel(tc, x, W_bytes, W_scale, out_0, out_1,
 
         w_cast(0, 0)
         w_cast(0, 1)
+        end_tables()
         w_turn(0, 0)
         w_turn(0, 1)
         x_turn(0, 0, 1)

@@ -21,17 +21,18 @@ FLOPS = 2 * B * L * D * 3 * H * DH
 P = 128
 NG = 12
 SEQ = (0, 4, 1, 5, 8, 2, 6, 9, 3, 10, 7, 11)
-S_HALF = (3, 4, 5, 6, 7, 8, 9, 10, 11)
+P_HALF = ((3, 1), (4, 1), (5, 1), (6, 1), (7, 1), (8, 1), (9, 1), (10, 1), (11, 1))
 G_WEAVE = ()
-Q0 = 2
-QNUM = 5
-QDEN = 2
+UNITS = ((0,), (1,), (2,), (3,), (4, 5), (6, 7), (8, 9), (10, 11))
+UNIT_Q = (None, 2, 4, 7, 11, 16, 21, 26)
+STAGGER = 2
+V_LAST = 1
 LEAD_MM = 2
 LEAD_T = 1
 LEAD_C = 3
 LEAD_W = 3
 LEAD_PL = 1
-V_ADDS = (31,)
+N_VADD = 1
 SPLIT_CASTS = 2
 TP_BUFS = 4
 ACC_BUFS = 4
@@ -205,11 +206,17 @@ def tile_multiheadselfattention_pa_kernel(tc, x, W_bytes, W_scale, out_0, out_1,
                     nc.tensor.transpose(tp[:, 128 * sl : 128 * (sl + 1)], ww[:, lo + u : lo + 256 : 2], ident[:])
             tp_of[(s, g)] = tp
 
+        unit_of = {}
+        for un, unit in enumerate(UNITS):
+            for m, s in enumerate(unit):
+                unit_of[s] = (un, m)
+
         def wg_half(s, g):
-            if s not in wg_of:
-                wg = wgp.tile([P, 2, 1024], BF16, name="wg", align_bytes=64)
-                wg_of[s] = wg
-            return wg_of[s][:, g, :]
+            un, m = unit_of[s]
+            if un not in wg_of:
+                wg = wgp.tile([P, 2, 2, 1024], BF16, name="wg", align_bytes=64)
+                wg_of[un] = wg
+            return wg_of[un][:, m, g, :]
 
         def w_scale(s, g):
             nc.vector.tensor_tensor(
@@ -230,25 +237,29 @@ def tile_multiheadselfattention_pa_kernel(tc, x, W_bytes, W_scale, out_0, out_1,
         def w_weave(s, g):
             dst = wg_half(s, g).rearrange("p (c t) -> p c t", t=4)
             src = pl_of[(s, g)][:].rearrange("p t c -> p c t")
-            if s in G_WEAVE:
+            if (s, g) in G_WEAVE:
                 nc.gpsimd.tensor_scalar(out=dst, in0=src, scalar1=1.0, scalar2=0.0, op0=ALU.mult, op1=ALU.add)
             else:
                 nc.scalar.copy(out=dst, in_=src)
 
-        def w_quant(s):
-            wc = wcp.tile([P, 512], U32, name="wc", align_bytes=64)
-            ws = wcp.tile([P, 512], U8, name="ws", align_bytes=64)
+        def w_quant(un):
+            n = len(UNITS[un])
+            wc = wcp.tile([P, 2, 512], U32, name="wc", align_bytes=64)
+            ws = wcp.tile([P, 2, 512], U8, name="ws", align_bytes=64)
             nc.vector.quantize_mx(
-                out=wc[:].bitcast(FP8X4), scales=ws[:], in_=wg_of[s][:].rearrange("p g c -> p (g c)")
+                out=wc[:, 0:n, :].rearrange("p m c -> p (m c)").bitcast(FP8X4),
+                scales=ws[:, 0:n, :].rearrange("p m c -> p (m c)"),
+                in_=wg_of[un][:, 0:n, :, :].rearrange("p m g c -> p (m g c)"),
             )
-            wc_of[s] = (wc, ws)
+            wc_of[un] = (wc, ws)
 
         acc_of = {}
         st_of = {}
         tb_of = {}
 
         def project(s, b, spare=False):
-            wc, ws = wc_of[s]
+            un, m = unit_of[s]
+            wc, ws = wc_of[un]
             if spare:
                 acc = psum_t.tile([P, 512], F32, name="tp")
             else:
@@ -262,8 +273,8 @@ def tile_multiheadselfattention_pa_kernel(tc, x, W_bytes, W_scale, out_0, out_1,
                         out=acc[:, 256 * j : 256 * (j + 1)],
                         lhsT=xc[:, b, xcols].bitcast(FP8X4),
                         lhsT_scale=xs[:, b, xcols],
-                        rhs=wc[:, wcols].bitcast(FP8X4),
-                        rhs_scale=ws[:, wcols],
+                        rhs=wc[:, m, wcols].bitcast(FP8X4),
+                        rhs_scale=ws[:, m, wcols],
                         start=(g == 0),
                         stop=(g == 1),
                     )
@@ -311,24 +322,24 @@ def tile_multiheadselfattention_pa_kernel(tc, x, W_bytes, W_scale, out_0, out_1,
         rope_banks = [(s, b) for s in range(NG) if SEQ[s] < 8 for b in range(B)]
         v_banks = [(s, b) for s in range(NG) if SEQ[s] >= 8 for b in range(B)]
         n_rope = len(rope_banks)
-        quant_at = {s: Q0 + (s - 1) * QNUM // QDEN for s in range(1, NG)}
+        quant_at = {s: UNIT_Q[unit_of[s][0]] for s in range(1, NG)}
         for r in range(B, n_rope):
             assert quant_at[rope_banks[r][0]] + LEAD_MM <= r
         scale_at = {}
         plane_at = {}
         weave_at = {}
         turn_at = {}
-        for s in range(1, NG):
-            if s in S_HALF:
-                scale_at[(s, 0)] = quant_at[s] - 1
-                weave_at[s] = quant_at[s] - LEAD_W
-                plane_at[s] = weave_at[s] - LEAD_PL
-                turn_at[(s, 1)] = plane_at[s] - LEAD_T
-            else:
-                scale_at[(s, 0)] = quant_at[s] - 2
-                scale_at[(s, 1)] = quant_at[s] - 1
-                turn_at[(s, 1)] = scale_at[(s, 1)] - LEAD_T
-            turn_at[(s, 0)] = scale_at[(s, 0)] - LEAD_T
+        for un in range(1, len(UNITS)):
+            halves = [(s, g) for s in UNITS[un] for g in range(2)]
+            v_halves = [hf for hf in halves if hf not in P_HALF]
+            p_halves = [hf for hf in halves if hf in P_HALF]
+            for n, hf in enumerate(reversed(v_halves)):
+                scale_at[hf] = UNIT_Q[un] - 1 - max(0, n - V_LAST + 1)
+                turn_at[hf] = scale_at[hf] - LEAD_T
+            for n, hf in enumerate(reversed(p_halves)):
+                weave_at[hf] = UNIT_Q[un] - LEAD_W - STAGGER * n
+                plane_at[hf] = weave_at[hf] - LEAD_PL
+                turn_at[hf] = plane_at[hf] - LEAD_T
         cast_at = {}
         for s in range(1, NG):
             for a in range(2):
@@ -371,7 +382,7 @@ def tile_multiheadselfattention_pa_kernel(tc, x, W_bytes, W_scale, out_0, out_1,
                         if cast_at[(s, a)] < first:
                             w_cast(s, a)
             for s in range(1, NG):
-                for g in (1, 0) if s in S_HALF else (0, 1):
+                for g in (1, 0) if turn_at[(s, 1)] < turn_at[(s, 0)] else (0, 1):
                     if due(turn_at[(s, g)], i):
                         w_turn(s, g)
             if i == -1:
@@ -382,11 +393,11 @@ def tile_multiheadselfattention_pa_kernel(tc, x, W_bytes, W_scale, out_0, out_1,
                 rope_sin(s, b)
                 if i + 1 < B:
                     x_quant(i + 1, 1)
-                for q in range(1, NG):
-                    if quant_at[q] == i:
-                        w_quant(q)
+                for un in range(1, len(UNITS)):
+                    if UNIT_Q[un] == i:
+                        w_quant(un)
                 rope_cos(s, b)
-                rope_add(s, b, nc.vector if i in V_ADDS else nc.gpsimd)
+                rope_add(s, b, nc.vector if i >= n_rope - N_VADD else nc.gpsimd)
             if 0 <= i and i + 1 < B:
                 project(rope_banks[i + 1][0], rope_banks[i + 1][1])
             for s in range(1, NG):
@@ -405,13 +416,13 @@ def tile_multiheadselfattention_pa_kernel(tc, x, W_bytes, W_scale, out_0, out_1,
                     store(v_banks[n][0], v_banks[n][1])
             if 0 <= i < n_rope:
                 store(rope_banks[i][0], rope_banks[i][1])
-            for s in S_HALF:
-                if due(plane_at[s], i):
+            for s, g in P_HALF:
+                if due(plane_at[(s, g)], i):
                     for t in range(4):
-                        w_plane(s, 1, t)
-            for s in S_HALF:
-                if due(weave_at[s], i):
-                    w_weave(s, 1)
+                        w_plane(s, g, t)
+            for s, g in P_HALF:
+                if due(weave_at[(s, g)], i):
+                    w_weave(s, g)
             for s in range(1, NG):
                 for a in range(2):
                     if cast_at[(s, a)] == i:

import math
from contextlib import ExitStack

import concourse.masks as masks
import concourse.mybir as mybir

F32 = mybir.dt.float32
BF16 = mybir.dt.bfloat16
I32 = mybir.dt.int32
U32 = mybir.dt.uint32
U8 = mybir.dt.uint8
FP8 = mybir.dt.float8_e4m3fn
FP8X4 = mybir.dt.float8_e4m3fn_x4
ALU = mybir.AluOpType
ACTF = mybir.ActivationFunctionType

B, L, D, H, DH = 4, 256, 1024, 16, 64
THETA = 100000.0
FLOPS = 2 * B * L * D * 3 * H * DH

P = 128
NG = 12
SEQ = (0, 4, 1, 5, 8, 2, 6, 9, 3, 10, 7, 11)
P_HALF = ((3, 1), (4, 1), (5, 1), (6, 1), (7, 1), (8, 1), (9, 1), (10, 1), (11, 1))
G_WEAVE = ()
UNITS = ((0,), (1,), (2,), (3,), (4, 5), (6, 7), (8, 9), (10, 11))
UNIT_Q = (None, 2, 4, 7, 11, 16, 21, 26)
STAGGER = 2
V_LAST = 1
LEAD_MM = 2
LEAD_T = 1
LEAD_C = 3
LEAD_W = 3
LEAD_PL = 1
N_VADD = 1
SPLIT_CASTS = 2
TP_BUFS = 4
ACC_BUFS = 4

TWO_PI = 2.0 * math.pi
C1 = 6.28125
C2 = 0.0019352436065673828
C3 = TWO_PI - C1 - C2


def tile_multiheadselfattention_pa_kernel(tc, x, W_bytes, W_scale, out_0, out_1, out_2):
    nc = tc.nc
    outs = (out_0, out_1, out_2)

    with ExitStack() as ctx:
        const = ctx.enter_context(tc.tile_pool(name="const", bufs=1))
        wbfp = ctx.enter_context(tc.tile_pool(name="wbfp", bufs=7))
        wgp = ctx.enter_context(tc.tile_pool(name="wgp", bufs=6))
        wcp = ctx.enter_context(tc.tile_pool(name="wcp", bufs=4))
        stp = ctx.enter_context(tc.tile_pool(name="stp", bufs=10))
        tbp = ctx.enter_context(tc.tile_pool(name="tbp", bufs=6))
        plp = ctx.enter_context(tc.tile_pool(name="plp", bufs=4))
        psum_t = ctx.enter_context(tc.psum_pool(name="psum_t", bufs=TP_BUFS))
        psum_a = ctx.enter_context(tc.psum_pool(name="psum_a", bufs=ACC_BUFS))
        ctx.enter_context(tc.manual_schedule())

        sc = const.tile([P, 2, 4], F32, name="sc")
        wbytes = const.tile([P, NG, 2048], U8, name="wbytes")
        x_sb = const.tile([P, B, 2048], BF16, name="x_sb")

        def load_w(s):
            gi = SEQ[s]
            nc.sync.dma_start(
                out=wbytes[:, gi, :],
                in_=W_bytes[256 * gi : 256 * (gi + 1), :].rearrange("(p a) k -> p (a k)", a=2),
            )

        def load_x(b):
            nc.sync.dma_start(out=x_sb[:, b, :], in_=x[b].rearrange("(p j) k -> p (j k)", j=2))

        for g in range(2):
            nc.sync.dma_start(
                out=wbytes[:, SEQ[0], :].rearrange("p (a k) -> p a k", a=2)[:, :, 512 * g : 512 * (g + 1)],
                in_=W_bytes[256 * SEQ[0] : 256 * (SEQ[0] + 1), 512 * g : 512 * (g + 1)].rearrange("(p a) k -> p a k", a=2),
            )
        nc.sync.dma_start(out=sc[:], in_=W_scale.rearrange("o (g p t) -> p (o g) t", g=2, p=P, t=4))
        load_x(0)
        load_x(1)
        load_w(1)
        load_x(2)
        load_x(3)
        for s in range(2, NG):
            load_w(s)

        posi = const.tile([P, 2], I32, name="posi")
        nc.gpsimd.iota(posi[:], pattern=[[1, 2]], base=0, channel_multiplier=2)
        ident = const.tile([P, P], F32, name="ident")
        masks.make_identity(nc, ident[:])
        zero = const.tile([P, 1], F32, name="zero")
        nc.vector.memset(zero[:], 0.0)
        warm = const.tile([P, 1], F32, name="warm")
        nc.scalar.activation(out=warm[:], in_=zero[:], func=ACTF.Sin)

        ang = const.tile([P, 2, 32], F32, name="ang")
        nc.vector.tensor_copy(out=ang[:, :, 0:1], in_=posi[:].unsqueeze(2))
        for w in (1, 2, 4, 8, 16):
            nc.vector.tensor_scalar(
                out=ang[:, :, w : 2 * w], in0=ang[:, :, 0:w], scalar1=THETA ** (-2.0 * w / DH), scalar2=None, op0=ALU.mult
            )
        angf = ang[:].rearrange("p j i -> p (j i)")
        ki = const.tile([P, 64], I32, name="ki")
        nc.vector.tensor_scalar(out=ki[:], in0=angf, scalar1=1.0 / TWO_PI, scalar2=None, op0=ALU.mult)
        kf = const.tile([P, 64], F32, name="kf")
        nc.vector.tensor_copy(out=kf[:], in_=ki[:])
        r1 = const.tile([P, 64], F32, name="r1")
        nc.vector.scalar_tensor_tensor(out=r1[:], in0=kf[:], scalar=-C1, in1=angf, op0=ALU.mult, op1=ALU.add)
        r2 = const.tile([P, 64], F32, name="r2")
        nc.vector.scalar_tensor_tensor(out=r2[:], in0=kf[:], scalar=-C2, in1=r1[:], op0=ALU.mult, op1=ALU.add)
        r3 = const.tile([P, 64], F32, name="r3")
        qc = const.tile([P, 64], F32, name="qc")
        s4 = const.tile([P, 64], F32, name="s4")
        c4 = const.tile([P, 64], F32, name="c4")
        ssgn = const.tile([P, 2, 32, 2], F32, name="ssgn")
        cdup = const.tile([P, 2, 32, 2], F32, name="cdup")
        cdup64 = cdup[:].rearrange("p j i e -> p j (i e)")
        sc2 = const.tile([P, 2, 2, 4], F32, name="sc2")
        sh = const.tile([P, 64], F32, name="sh")
        q2 = const.tile([P, 64], F32, name="q2")
        c2 = const.tile([P, 64], F32, name="c2")
        sq = const.tile([P, 2, 32], F32, name="sq")
        q1 = const.tile([P, 2, 32], F32, name="q1")

        def end_tables():
            nc.vector.scalar_tensor_tensor(out=r3[:], in0=kf[:], scalar=-C3, in1=r2[:], op0=ALU.mult, op1=ALU.add)
            nc.vector.tensor_scalar(out=qc[:], in0=r3[:], scalar1=0.25, scalar2=0.5 * math.pi, op0=ALU.mult, op1=ALU.add)
            nc.scalar.activation(out=s4[:], in_=r3[:], func=ACTF.Sin, scale=0.25)
            nc.scalar.activation(out=c4[:], in_=qc[:], func=ACTF.Sin)
            nc.gpsimd.tensor_tensor(out=sh[:], in0=s4[:], in1=c4[:], op=ALU.mult)
            nc.gpsimd.tensor_tensor(out=q2[:], in0=s4[:], in1=s4[:], op=ALU.mult)
            nc.gpsimd.tensor_scalar(out=c2[:], in0=q2[:], scalar1=-2.0, scalar2=1.0, op0=ALU.mult, op1=ALU.add)
            nc.gpsimd.tensor_tensor(out=sq[:].rearrange("p j i -> p (j i)"), in0=sh[:], in1=c2[:], op=ALU.mult)
            nc.gpsimd.tensor_scalar(
                out=ssgn[:, :, :, 0:1], in0=sq[:].unsqueeze(3), scalar1=-4.0, scalar2=0.0, op0=ALU.mult, op1=ALU.add
            )
            nc.gpsimd.tensor_scalar(
                out=ssgn[:, :, :, 1:2], in0=sq[:].unsqueeze(3), scalar1=4.0, scalar2=0.0, op0=ALU.mult, op1=ALU.add
            )
            nc.gpsimd.tensor_tensor(out=q1[:].rearrange("p j i -> p (j i)"), in0=sh[:], in1=sh[:], op=ALU.mult)
            nc.gpsimd.tensor_scalar(
                out=cdup[:],
                in0=q1[:].unsqueeze(3).to_broadcast([P, 2, 32, 2]),
                scalar1=-8.0,
                scalar2=1.0,
                op0=ALU.mult,
                op1=ALU.add,
            )

        xg = const.tile([P, B, 2, 1024], BF16, name="xg", align_bytes=64)
        xc = const.tile([P, B, 512], U32, name="xc", align_bytes=64)
        xs = const.tile([P, B, 512], U8, name="xs", align_bytes=64)

        def x_turn(b, j, eng):
            tp = psum_t.tile([P, 512], F32, name="tp")
            xw = x_sb[:, b, 1024 * j : 1024 * (j + 1)].bitcast(F32)
            for g in range(2):
                for u in range(2):
                    sl = 2 * g + u
                    nc.tensor.transpose(
                        tp[:, 128 * sl : 128 * (sl + 1)], xw[:, 256 * g + u : 256 * (g + 1) : 2], ident[:]
                    )
            dst = xg[:, b, :, 512 * j : 512 * (j + 1)].bitcast(F32).rearrange("p g (r u) -> p g r u", u=2)
            src = tp[:].rearrange("p (g u r) -> p g r u", g=2, u=2)
            if eng == 0:
                nc.vector.tensor_copy(out=dst, in_=src)
            else:
                nc.scalar.copy(out=dst, in_=src)

        def x_quant(b, n):
            nc.vector.quantize_mx(
                out=xc[:, b : b + n, :].rearrange("p b c -> p (b c)").bitcast(FP8X4),
                scales=xs[:, b : b + n, :].rearrange("p b c -> p (b c)"),
                in_=xg[:, b : b + n, :, :].rearrange("p b g c -> p (b g c)"),
            )

        wbf_of = {}
        tp_of = {}
        wg_of = {}
        wc_of = {}
        pl_of = {}

        def w_cast(s, a):
            if a == 0:
                wbf_new = wbfp.tile([P, 2048], BF16, name="wbf")
                wbf_of[s] = wbf_new
            wbf = wbf_of[s]
            src = wbytes[:, SEQ[s], :].bitcast(FP8)
            lo = 1024 * a
            if s < SPLIT_CASTS:
                nc.vector.tensor_copy(out=wbf[:, lo : lo + 512], in_=src[:, lo : lo + 512])
                nc.scalar.copy(out=wbf[:, lo + 512 : lo + 1024], in_=src[:, lo + 512 : lo + 1024])
            else:
                nc.scalar.copy(out=wbf[:, lo : lo + 1024], in_=src[:, lo : lo + 1024])

        def w_turn(s, g):
            ww = wbf_of[s][:].bitcast(F32)
            tp = psum_t.tile([P, 512], F32, name="tp")
            for a in range(2):
                for u in range(2):
                    sl = 2 * a + u
                    lo = 512 * a + 256 * g
                    nc.tensor.transpose(tp[:, 128 * sl : 128 * (sl + 1)], ww[:, lo + u : lo + 256 : 2], ident[:])
            tp_of[(s, g)] = tp

        unit_of = {}
        for un, unit in enumerate(UNITS):
            for m, s in enumerate(unit):
                unit_of[s] = (un, m)

        def wg_half(s, g):
            un, m = unit_of[s]
            if un not in wg_of:
                wg = wgp.tile([P, 2, 2, 1024], BF16, name="wg", align_bytes=64)
                wg_of[un] = wg
            return wg_of[un][:, m, g, :]

        def w_scale(s, g):
            nc.vector.tensor_tensor(
                out=wg_half(s, g).rearrange("p (r q e) -> p r q e", q=4, e=2),
                in0=tp_of[(s, g)][:].bitcast(BF16).rearrange("p (q r e) -> p r q e", q=4, e=2),
                in1=sc2[:, g, :, :].rearrange("p a (u e) -> p (a u) e", e=2).unsqueeze(1).to_broadcast([P, 128, 4, 2]),
                op=ALU.mult,
            )

        def w_plane(s, g, t):
            if t == 0:
                pl = plp.tile([P, 4, 256], BF16, name="pl")
                pl_of[(s, g)] = pl
            src = tp_of[(s, g)][:].bitcast(BF16).rearrange("p (a u r e) -> p u e r a", a=2, u=2, e=2)
            dst = pl_of[(s, g)][:, t, :].rearrange("p (r a) -> p r a", a=2)
            nc.scalar.activation(out=dst, in_=src[:, t // 2, t % 2], func=ACTF.Copy, scale=sc[:, g, t : t + 1])

        def w_weave(s, g):
            dst = wg_half(s, g).rearrange("p (c t) -> p c t", t=4)
            src = pl_of[(s, g)][:].rearrange("p t c -> p c t")
            if (s, g) in G_WEAVE:
                nc.gpsimd.tensor_scalar(out=dst, in0=src, scalar1=1.0, scalar2=0.0, op0=ALU.mult, op1=ALU.add)
            else:
                nc.scalar.copy(out=dst, in_=src)

        def w_quant(un):
            n = len(UNITS[un])
            wc = wcp.tile([P, 2, 512], U32, name="wc", align_bytes=64)
            ws = wcp.tile([P, 2, 512], U8, name="ws", align_bytes=64)
            nc.vector.quantize_mx(
                out=wc[:, 0:n, :].rearrange("p m c -> p (m c)").bitcast(FP8X4),
                scales=ws[:, 0:n, :].rearrange("p m c -> p (m c)"),
                in_=wg_of[un][:, 0:n, :, :].rearrange("p m g c -> p (m g c)"),
            )
            wc_of[un] = (wc, ws)

        acc_of = {}
        st_of = {}
        tb_of = {}

        def project(s, b, spare=False):
            un, m = unit_of[s]
            wc, ws = wc_of[un]
            if spare:
                acc = psum_t.tile([P, 512], F32, name="tp")
            else:
                acc = psum_a.tile([P, 512], F32, name="acc")
            acc_of[(s, b)] = acc
            for j in range(2):
                for g in range(2):
                    xcols = slice(256 * g + 128 * j, 256 * g + 128 * (j + 1))
                    wcols = slice(256 * g, 256 * (g + 1))
                    nc.tensor.matmul_mx(
                        out=acc[:, 256 * j : 256 * (j + 1)],
                        lhsT=xc[:, b, xcols].bitcast(FP8X4),
                        lhsT_scale=xs[:, b, xcols],
                        rhs=wc[:, m, wcols].bitcast(FP8X4),
                        rhs_scale=ws[:, m, wcols],
                        start=(g == 0),
                        stop=(g == 1),
                    )

        def store(s, b):
            gi = SEQ[s]
            h0 = 4 * (gi % 4)
            nc.sync.dma_start(
                out=outs[gi // 4][b, h0 : h0 + 4, :, :].rearrange("h (p j) d -> p h (j d)", j=2),
                in_=st_of[(s, b)][:].rearrange("p h j d -> p h (j d)"),
            )

        def v_out(s, b):
            stage = stp.tile([P, 4, 2, 64], F32, name="stage")
            st_of[(s, b)] = stage
            nc.scalar.copy(
                out=stage[:].rearrange("p h j d -> p j h d"),
                in_=acc_of[(s, b)][:].rearrange("p (j h d) -> p j h d", j=2, h=4),
            )

        def rope_sin(s, b):
            tb = tbp.tile([P, 4, 2, 64], F32, name="tb")
            tb_of[(s, b)] = tb
            nc.vector.tensor_tensor(
                out=tb[:].rearrange("p h j (i e) -> p j h i e", e=2),
                in0=acc_of[(s, b)][:].rearrange("p (j h i e) -> p j h i e", j=2, h=4, e=2)[:, :, :, :, ::-1],
                in1=ssgn[:].unsqueeze(2).to_broadcast([P, 2, 4, 32, 2]),
                op=ALU.mult,
            )

        def rope_cos(s, b):
            stage = stp.tile([P, 4, 2, 64], F32, name="stage")
            st_of[(s, b)] = stage
            nc.vector.tensor_tensor(
                out=stage[:].rearrange("p h j d -> p j h d"),
                in0=acc_of[(s, b)][:].rearrange("p (j h d) -> p j h d", j=2, h=4),
                in1=cdup64.unsqueeze(2).to_broadcast([P, 2, 4, 64]),
                op=ALU.mult,
            )

        def rope_add(s, b, eng):
            st_flat = st_of[(s, b)][:].rearrange("p h j d -> p (h j d)")
            eng.tensor_tensor(out=st_flat, in0=st_flat, in1=tb_of[(s, b)][:].rearrange("p h j d -> p (h j d)"), op=ALU.add)

        rope_banks = [(s, b) for s in range(NG) if SEQ[s] < 8 for b in range(B)]
        v_banks = [(s, b) for s in range(NG) if SEQ[s] >= 8 for b in range(B)]
        n_rope = len(rope_banks)
        quant_at = {s: UNIT_Q[unit_of[s][0]] for s in range(1, NG)}
        for r in range(B, n_rope):
            assert quant_at[rope_banks[r][0]] + LEAD_MM <= r
        scale_at = {}
        plane_at = {}
        weave_at = {}
        turn_at = {}
        for un in range(1, len(UNITS)):
            halves = [(s, g) for s in UNITS[un] for g in range(2)]
            v_halves = [hf for hf in halves if hf not in P_HALF]
            p_halves = [hf for hf in halves if hf in P_HALF]
            for n, hf in enumerate(reversed(v_halves)):
                scale_at[hf] = UNIT_Q[un] - 1 - max(0, n - V_LAST + 1)
                turn_at[hf] = scale_at[hf] - LEAD_T
            for n, hf in enumerate(reversed(p_halves)):
                weave_at[hf] = UNIT_Q[un] - LEAD_W - STAGGER * n
                plane_at[hf] = weave_at[hf] - LEAD_PL
                turn_at[hf] = plane_at[hf] - LEAD_T
        cast_at = {}
        for s in range(1, NG):
            for a in range(2):
                cast_at[(s, a)] = min(turn_at[(s, 0)], turn_at[(s, 1)]) - LEAD_C + a
        v_two = 1 + max(turn_at.values())
        v_at = []
        for s, b in v_banks:
            soonest = quant_at[s] + 1
            if len(v_at) >= 2 and v_at[-1] >= v_two:
                v_at.append(max(soonest, v_at[-2] + 1))
            elif v_at:
                v_at.append(max(soonest, v_at[-1] + 1))
            else:
                v_at.append(soonest)
        last = max(n_rope, v_at[-1] + 1)
        first = -2

        def due(at, i):
            return at == i or (i == first and at < first)

        w_cast(0, 0)
        w_cast(0, 1)
        end_tables()
        w_turn(0, 0)
        w_turn(0, 1)
        x_turn(0, 0, 1)
        x_turn(0, 1, 1)
        nc.vector.tensor_copy(out=sc2[:], in_=sc[:].unsqueeze(2).to_broadcast([P, 2, 2, 4]))
        w_scale(0, 0)
        w_scale(0, 1)
        x_turn(1, 0, 1)
        x_turn(1, 1, 1)
        w_quant(0)
        x_quant(0, 1)
        project(rope_banks[0][0], rope_banks[0][1])
        for i in range(first, last):
            if i == first:
                for s in range(1, NG):
                    for a in range(2):
                        if cast_at[(s, a)] < first:
                            w_cast(s, a)
            for s in range(1, NG):
                for g in (1, 0) if turn_at[(s, 1)] < turn_at[(s, 0)] else (0, 1):
                    if due(turn_at[(s, g)], i):
                        w_turn(s, g)
            if i == -1:
                x_turn(2, 0, 1)
                x_turn(2, 1, 1)
            if 0 <= i < n_rope:
                s, b = rope_banks[i]
                rope_sin(s, b)
                if i + 1 < B:
                    x_quant(i + 1, 1)
                for un in range(1, len(UNITS)):
                    if UNIT_Q[un] == i:
                        w_quant(un)
                rope_cos(s, b)
                rope_add(s, b, nc.vector if i >= n_rope - N_VADD else nc.gpsimd)
            if 0 <= i and i + 1 < B:
                project(rope_banks[i + 1][0], rope_banks[i + 1][1])
            for s in range(1, NG):
                for g in range(2):
                    if (s, g) in scale_at and scale_at[(s, g)] == i:
                        w_scale(s, g)
            if i == 0:
                x_turn(3, 0, 1)
                x_turn(3, 1, 1)
            if 2 <= i and i + LEAD_MM < n_rope:
                project(rope_banks[i + LEAD_MM][0], rope_banks[i + LEAD_MM][1])
            for n, at in enumerate(v_at):
                if at == i:
                    project(v_banks[n][0], v_banks[n][1], i >= v_two)
                    v_out(v_banks[n][0], v_banks[n][1])
                    store(v_banks[n][0], v_banks[n][1])
            if 0 <= i < n_rope:
                store(rope_banks[i][0], rope_banks[i][1])
            for s, g in P_HALF:
                if due(plane_at[(s, g)], i):
                    for t in range(4):
                        w_plane(s, g, t)
            for s, g in P_HALF:
                if due(weave_at[(s, g)], i):
                    w_weave(s, g)
            for s in range(1, NG):
                for a in range(2):
                    if cast_at[(s, a)] == i:
                        w_cast(s, a)
